import numpy as np
import ml_dtypes


def mxq(x, axis, fmt="e4m3"):
    dtype, down = {"e4m3": (ml_dtypes.float8_e4m3fn, 7), "e5m2": (ml_dtypes.float8_e5m2, 14)}[fmt]
    v = np.moveaxis(np.asarray(x, np.float32).astype(ml_dtypes.bfloat16).astype(np.float64), axis, -1)
    blocks = v.reshape(v.shape[:-1] + (-1, 32))
    amax = np.abs(blocks).max(-1, keepdims=True)
    byte = np.maximum(np.where(amax > 0, np.frexp(amax)[1] - 1 + 127, 0) - down, 1)
    scale = np.exp2(byte - 127.0)
    codes = (blocks / scale).astype(np.float32).astype(dtype).astype(np.float64)
    return np.moveaxis((codes * scale).reshape(v.shape), -1, axis)


WIDE = False


def mx_kscale(k):
    if not WIDE:
        return np.ones(k)
    levels = np.array([10, -10, 5, -5, 0])
    if k % 512:
        return np.exp2(np.random.permutation(np.resize(levels, k // 32))).repeat(32)
    a = np.empty((k // 512, 16))
    for p in range(k // 512):
        a[p, :8] = np.random.permutation(np.resize(levels, 8))
        for g in range(8):
            far = levels[np.abs(levels - a[p, g]) >= 10]
            a[p, g + 8] = far[np.random.randint(len(far))]
    return np.exp2(a.ravel()).repeat(32)


BF16 = ml_dtypes.bfloat16


def bf(x):
    return np.asarray(x, np.float32).astype(BF16)


def f64(x):
    return np.asarray(x).astype(np.float64)


B, S, H, HD = 4, 2048, 4, 128
DIM = H * HD


def setup_inputs():
    s, t = mx_kscale(DIM), mx_kscale(DIM)
    return {"x": bf(np.random.standard_normal((B, S, DIM)) * 2.0 * s),
            "y_norm": bf(np.random.standard_normal((B, S, DIM))),
            "wg_w": bf(np.random.standard_normal((DIM, DIM)) * 0.5 / np.sqrt(DIM) / s[:, None] * t),
            "wo_w": bf(np.random.standard_normal((DIM, DIM)) * 1.5 / np.sqrt(DIM) / t[:, None])}


def reference(x, y_norm, wg_w, wo_w):
    g = np.maximum(mxq(f64(x), 2, "e4m3") @ mxq(f64(wg_w), 0, "e4m3"), 0.0)
    h = g * f64(y_norm)
    return mxq(h, 2, "e4m3") @ mxq(f64(wo_w), 0, "e4m3")

@@ -1,0 +1,310 @@
+from contextlib import ExitStack
+
+import concourse.mybir as mybir
+from concourse.masks import make_identity
+
+F32 = mybir.dt.float32
+BF16 = mybir.dt.bfloat16
+U32 = mybir.dt.uint32
+U8 = mybir.dt.uint8
+FP8X4 = mybir.dt.float8_e4m3fn_x4
+ALU = mybir.AluOpType
+
+P = 128
+D = 512
+H = D // 2
+TOKENS = 8192
+FLOPS = 2 * 2 * TOKENS * D * D
+
+G_DT = F32
+
+CHUNK_TILES = [2, 2, 4] + [8] * 7
+GROUP_UNITS = [1, 1] + [2] * 14 + [1, 1]
+BULK = 8
+BULK_BUFS = 3
+OUT_BUFS = 3
+HEAD_LOADS = ["x0","wg","x1","y0","x2","wo","y1","x3","y2"]
+TAIL_SPLIT = 2
+
+
+def tile_multiscaleretention_pb_t_kernel(tc, x, y_norm, wg_w, wo_w, out):
+    nc = tc.nc
+    xf = x.flatten_outer_dims()
+    yf = y_norm.flatten_outer_dims()
+    of = out.flatten_outer_dims()
+
+    chunk_start = []
+    units = []
+    t0 = 0
+    for c, tiles in enumerate(CHUNK_TILES):
+        chunk_start.append(t0)
+        for j0 in range(0, tiles, 2):
+            units.append((c, j0))
+        t0 += P * tiles
+    assert t0 == TOKENS
+    last_unit_of_chunk = {}
+    for U, (c, j0) in enumerate(units):
+        last_unit_of_chunk[c] = U
+    groups = []
+    group_of = {}
+    for size in GROUP_UNITS:
+        first = sum(len(g) for g in groups)
+        groups.append(list(range(first, first + size)))
+        for U in groups[-1]:
+            group_of[U] = (len(groups) - 1, U - first)
+    assert sum(GROUP_UNITS) == len(units)
+    n_groups = len(groups)
+
+    def members(G):
+        return groups[G] if 0 <= G < n_groups else []
+
+    def dram_rows(flat, c):
+        tiles = CHUNK_TILES[c]
+        rows = flat[chunk_start[c] : chunk_start[c] + P * tiles, :]
+        return rows.rearrange("(p j) d -> p j d", j=tiles)
+
+    with ExitStack() as ctx:
+        const = ctx.enter_context(tc.tile_pool(name="const", bufs=1))
+        xin = ctx.enter_context(tc.tile_pool(name="xin", bufs=1))
+        yin = ctx.enter_context(tc.tile_pool(name="yin", bufs=1))
+        work = ctx.enter_context(tc.tile_pool(name="work", bufs=3))
+        outp = ctx.enter_context(tc.tile_pool(name="outp", bufs=OUT_BUFS))
+        psum = ctx.enter_context(tc.psum_pool(name="psum", bufs=2))
+        ctx.enter_context(tc.manual_schedule())
+
+        x_sb = {}
+        y_sb = {}
+        xt_ps = {}
+        xg = {}
+        xq = {}
+        g_ps = {}
+        h_sb = {}
+        ht_ps = {}
+        hg = {}
+        hq = {}
+        o_ps = {}
+        o_sb = {}
+
+        def load(pool, table, flat, c, letter):
+            tiles = CHUNK_TILES[c]
+            if tiles == BULK:
+                t = pool.tile([P, tiles, D], BF16, name="%sb" % letter, tag="%sb" % letter, bufs=BULK_BUFS)
+            else:
+                t = pool.tile([P, tiles, D], BF16, name="%sh%d" % (letter, c), tag="%sh%d" % (letter, c), bufs=1)
+            nc.sync.dma_start(out=t[:], in_=dram_rows(flat, c))
+            table[c] = t
+
+        def load_x(c):
+            if c < len(CHUNK_TILES):
+                load(xin, x_sb, xf, c, "x")
+
+        def load_y(c):
+            if c < len(CHUNK_TILES):
+                load(yin, y_sb, yf, c, "y")
+
+        def copy_on(engine, dst, src):
+            if engine == "V":
+                nc.vector.tensor_copy(out=dst, in_=src)
+            else:
+                nc.scalar.copy(out=dst, in_=src)
+
+        def transpose_x(U):
+            c, j0 = units[U]
+            ps = psum.tile([P, 2, 2, P], F32, name="xt_ps", tag="xt", bufs=2)
+            for jj in range(2):
+                words = x_sb[c][:, j0 + jj, :].bitcast(F32)
+                for u in range(2):
+                    nc.tensor.transpose(ps[:, jj, u, :], words[:, u:H:2], ident[:])
+            xt_ps[U] = ps
+            if U == last_unit_of_chunk[c] and CHUNK_TILES[c] == BULK:
+                load_x(c + BULK_BUFS)
+
+        def ungroup(engine, ps, table, tag, U):
+            G, k = group_of[U]
+            if k == 0:
+                table[G] = work.tile([P, len(groups[G]) * 8 * P], BF16, name=tag, tag=tag, bufs=3, align_bytes=64)
+            copy_on(
+                engine,
+                table[G][:, k * 8 * P : (k + 1) * 8 * P].bitcast(F32).rearrange("p (j r u) -> p j r u", j=2, u=2),
+                ps[:].rearrange("p j u r -> p j r u"),
+            )
+
+        def quantize(grouped, tag, G):
+            width = len(groups[G]) * 2 * P
+            codes = work.tile([P, width], U32, name=tag + "c", tag=tag + "c", bufs=3, align_bytes=64)
+            scales = work.tile([P, width], U8, name=tag + "s", tag=tag + "s", bufs=3, align_bytes=64)
+            nc.vector.quantize_mx(out=codes[:].bitcast(FP8X4), scales=scales[:], in_=grouped[:])
+            return codes, scales
+
+        def stage1(U, u):
+            G, k = group_of[U]
+            codes, scales = xq[G]
+            g = psum.tile([P, 2, H], G_DT, name="g_ps", tag="g", bufs=2)
+            half = slice(u * H, (u + 1) * H)
+            for jj in range(2):
+                cols = slice((2 * k + jj) * P, (2 * k + jj + 1) * P)
+                nc.tensor.matmul_mx(
+                    out=g[:, jj, :],
+                    lhsT=codes[:, cols].bitcast(FP8X4),
+                    lhsT_scale=scales[:, cols],
+                    rhs=wgc[:, half].bitcast(FP8X4),
+                    rhs_scale=wgs[:, half],
+                    start=True,
+                    stop=True,
+                )
+            g_ps[(U, u)] = g
+
+        def gate(U, u):
+            c, j0 = units[U]
+            if u == 0:
+                h_sb[U] = work.tile([P, 2, D], BF16, name="h_sb", tag="h", bufs=5, align_bytes=64)
+            y_pairs = (
+                y_sb[c][:, j0 : j0 + 2, :]
+                .rearrange("p j d -> p (j d)")
+                .rearrange("p (m u e) -> p u m e", u=2, e=2)
+            )
+            nc.vector.scalar_tensor_tensor(
+                out=h_sb[U][:, u, :].rearrange("p (m e) -> p m e", e=2),
+                in0=g_ps[(U, u)][:].rearrange("p j d -> p (j d)").rearrange("p (m e) -> p m e", e=2),
+                scalar=0.0,
+                in1=y_pairs[:, u],
+                op0=ALU.max,
+                op1=ALU.mult,
+            )
+            if u == 1 and U == last_unit_of_chunk[c] and CHUNK_TILES[c] == BULK:
+                load_y(c + BULK_BUFS)
+
+        def transpose_h(U):
+            ps = psum.tile([P, 2, 2, P], F32, name="ht_ps", tag="ht", bufs=2)
+            for jj in range(2):
+                for u in range(2):
+                    words = h_sb[U][:, u, jj * H : (jj + 1) * H].bitcast(F32)
+                    nc.tensor.transpose(ps[:, jj, u, :], words, ident[:])
+            ht_ps[U] = ps
+
+        def stage2(U, jj):
+            G, k = group_of[U]
+            codes, scales = hq[G]
+            o = psum.tile([P, D], F32, name="o_ps", tag="o", bufs=2)
+            cols = slice((2 * k + jj) * P, (2 * k + jj + 1) * P)
+            nc.tensor.matmul_mx(
+                out=o[:],
+                lhsT=codes[:, cols].bitcast(FP8X4),
+                lhsT_scale=scales[:, cols],
+                rhs=woc[:].bitcast(FP8X4),
+                rhs_scale=wos[:],
+                start=True,
+                stop=True,
+            )
+            o_ps[(U, jj)] = o
+
+        def copy_out(U, jj, engine):
+            G, k = group_of[U]
+            if k == 0 and jj == 0:
+                o_sb[G] = outp.tile([P, 2 * len(groups[G]), D], F32, name="o_sb", tag="o_sb", bufs=OUT_BUFS)
+            copy_on(engine, o_sb[G][:, 2 * k + jj, :], o_ps[(U, jj)][:])
+
+        def store(U, jj, count):
+            c, j0 = units[U]
+            G, k = group_of[U]
+            nc.sync.dma_start(
+                out=dram_rows(of, c)[:, j0 + jj : j0 + jj + count, :],
+                in_=o_sb[G][:, 2 * k + jj : 2 * k + jj + count, :],
+            )
+
+        wg_raw = const.tile([P, 4, D], BF16, name="wg_raw")
+        wo_raw = const.tile([P, 4, D], BF16, name="wo_raw")
+        for what in HEAD_LOADS:
+            if what == "wg":
+                nc.sync.dma_start(out=wg_raw[:], in_=wg_w.rearrange("(p j) c -> p j c", j=4))
+            elif what == "wo":
+                nc.sync.dma_start(out=wo_raw[:], in_=wo_w.rearrange("(p j) c -> p j c", j=4))
+            elif what.startswith("x"):
+                load_x(int(what[1:]))
+            else:
+                load_y(int(what[1:]))
+        for c in range(3, 3 + BULK_BUFS):
+            if c not in x_sb:
+                load_x(c)
+            if c not in y_sb:
+                load_y(c)
+
+        ident = const.tile([P, P], F32, name="ident")
+        make_identity(nc, ident[:])
+        warm = const.tile([P, 2], F32, name="warm")
+        nc.vector.memset(warm[:, 0:1], 0.0)
+        nc.scalar.copy(out=warm[:, 1:2], in_=warm[:, 0:1])
+
+        wg_grp = const.tile([P, 4 * D], BF16, name="wg_grp", align_bytes=64)
+        wgc = const.tile([P, D], U32, name="wgc", align_bytes=64)
+        wgs = const.tile([P, D], U8, name="wgs", align_bytes=64)
+        wo_grp = const.tile([P, 4 * D], BF16, name="wo_grp", align_bytes=64)
+        woc = const.tile([P, D], U32, name="woc", align_bytes=64)
+        wos = const.tile([P, D], U8, name="wos", align_bytes=64)
+
+        def group_wg(u, engine):
+            copy_on(
+                engine,
+                wg_grp[:, u * 2 * D : (u + 1) * 2 * D].rearrange("p (q e j) -> p q e j", e=2, j=4),
+                wg_raw[:].rearrange("p j (q u e) -> p u q e j", u=2, e=2)[:, u],
+            )
+
+        def quantize_wg(u):
+            nc.vector.quantize_mx(
+                out=wgc[:, u * H : (u + 1) * H].bitcast(FP8X4),
+                scales=wgs[:, u * H : (u + 1) * H],
+                in_=wg_grp[:, u * 2 * D : (u + 1) * 2 * D],
+            )
+
+        def group_wo(half, engine):
+            copy_on(
+                engine,
+                wo_grp[:, half * 2 * D : (half + 1) * 2 * D].rearrange("p (n j) -> p n j", j=4),
+                wo_raw[:, :, half * H : (half + 1) * H].rearrange("p j n -> p n j"),
+            )
+
+        for n in range(-1, n_groups + 2):
+            if members(n):
+                xq[n] = quantize(xg[n], "x", n)
+            if n == 0:
+                quantize_wg(0)
+                quantize_wg(1)
+            if n == 2:
+                nc.vector.quantize_mx(out=woc[:].bitcast(FP8X4), scales=wos[:], in_=wo_grp[:])
+            if members(n - 2):
+                hq[n - 2] = quantize(hg[n - 2], "h", n - 2)
+            nxt = members(n + 1)
+            prv = members(n - 1)
+            if nxt:
+                transpose_x(nxt[0])
+                ungroup("S", xt_ps[nxt[0]], xg, "xg", nxt[0])
+            if n == -1:
+                group_wg(0, "V")
+                group_wg(1, "S")
+            for U in prv:
+                transpose_h(U)
+                ungroup("V" if U == prv[-1] else "S", ht_ps[U], hg, "hg", U)
+            for U in nxt[1:]:
+                transpose_x(U)
+                ungroup("S", xt_ps[U], xg, "xg", U)
+            if n == 1:
+                group_wo(0, "S")
+                group_wo(1, "V")
+            banks = [(U, u) for U in members(n) for u in range(2)]
+            tiles = [(U, jj) for U in members(n - 2) for jj in range(2)]
+            drain = n - 2 >= n_groups - TAIL_SPLIT
+            for step in range(max(len(banks), len(tiles))):
+                if step < len(banks):
+                    stage1(banks[step][0], banks[step][1])
+                    gate(banks[step][0], banks[step][1])
+                if step < len(tiles):
+                    U, jj = tiles[step]
+                    stage2(U, jj)
+                    copy_out(U, jj, "V" if (drain and step % 2 == 1) else "S")
+                    whole = units[tiles[0][0]][0] == units[tiles[-1][0]][0]
+                    if n - 2 == n_groups - 1:
+                        store(U, jj, 1)
+                    elif whole and step == len(tiles) - 1:
+                        store(tiles[0][0], 0, len(tiles))
+                    elif not whole and jj == 1:
+                        store(U, 0, 2)

@@ -22,7 +22,7 @@ CHUNK_TILES = [2, 2, 4] + [8] * 7
 GROUP_UNITS = [1, 1] + [2] * 14 + [1, 1]
 BULK = 8
 BULK_BUFS = 3
-OUT_BUFS = 3
+OUT_BUFS = 4
 HEAD_LOADS = ["x0","wg","x1","y0","x2","wo","y1","x3","y2"]
 TAIL_SPLIT = 2
 
@@ -110,7 +110,7 @@ def tile_multiscaleretention_pb_t_kernel(tc, x, y_norm, wg_w, wo_w, out):
 
         def transpose_x(U):
             c, j0 = units[U]
-            ps = psum.tile([P, 2, 2, P], F32, name="xt_ps", tag="xt", bufs=2)
+            ps = psum.tile([P, 2, 2, P], F32, name="xt_ps", tag="bank", bufs=8)
             for jj in range(2):
                 words = x_sb[c][:, j0 + jj, :].bitcast(F32)
                 for u in range(2):
@@ -139,7 +139,7 @@ def tile_multiscaleretention_pb_t_kernel(tc, x, y_norm, wg_w, wo_w, out):
         def stage1(U, u):
             G, k = group_of[U]
             codes, scales = xq[G]
-            g = psum.tile([P, 2, H], G_DT, name="g_ps", tag="g", bufs=2)
+            g = psum.tile([P, 2, H], G_DT, name="g_ps", tag="bank", bufs=8)
             half = slice(u * H, (u + 1) * H)
             for jj in range(2):
                 cols = slice((2 * k + jj) * P, (2 * k + jj + 1) * P)
@@ -175,7 +175,7 @@ def tile_multiscaleretention_pb_t_kernel(tc, x, y_norm, wg_w, wo_w, out):
                 load_y(c + BULK_BUFS)
 
         def transpose_h(U):
-            ps = psum.tile([P, 2, 2, P], F32, name="ht_ps", tag="ht", bufs=2)
+            ps = psum.tile([P, 2, 2, P], F32, name="ht_ps", tag="bank", bufs=8)
             for jj in range(2):
                 for u in range(2):
                     words = h_sb[U][:, u, jj * H : (jj + 1) * H].bitcast(F32)
@@ -185,7 +185,7 @@ def tile_multiscaleretention_pb_t_kernel(tc, x, y_norm, wg_w, wo_w, out):
         def stage2(U, jj):
             G, k = group_of[U]
             codes, scales = hq[G]
-            o = psum.tile([P, D], F32, name="o_ps", tag="o", bufs=2)
+            o = psum.tile([P, D], F32, name="o_ps", tag="bank", bufs=8)
             cols = slice((2 * k + jj) * P, (2 * k + jj + 1) * P)
             nc.tensor.matmul_mx(
                 out=o[:],
@@ -223,7 +223,7 @@ def tile_multiscaleretention_pb_t_kernel(tc, x, y_norm, wg_w, wo_w, out):
                 load_x(int(what[1:]))
             else:
                 load_y(int(what[1:]))
-        for c in range(3, 3 + BULK_BUFS):
+        for c in range(CHUNK_TILES.index(BULK), CHUNK_TILES.index(BULK) + BULK_BUFS):
             if c not in x_sb:
                 load_x(c)
             if c not in y_sb:
@@ -283,7 +283,7 @@ def tile_multiscaleretention_pb_t_kernel(tc, x, y_norm, wg_w, wo_w, out):
                 group_wg(1, "S")
             for U in prv:
                 transpose_h(U)
-                ungroup("V" if U == prv[-1] else "S", ht_ps[U], hg, "hg", U)
+                ungroup("V" if (U == prv[-1] and n > 3) else "S", ht_ps[U], hg, "hg", U)
             for U in nxt[1:]:
                 transpose_x(U)
                 ungroup("S", xt_ps[U], xg, "xg", U)
@@ -302,8 +302,11 @@ def tile_multiscaleretention_pb_t_kernel(tc, x, y_norm, wg_w, wo_w, out):
                     stage2(U, jj)
                     copy_out(U, jj, "V" if (drain and step % 2 == 1) else "S")
                     whole = units[tiles[0][0]][0] == units[tiles[-1][0]][0]
-                    if n - 2 == n_groups - 1:
+                    if n - 2 >= n_groups - 1:
                         store(U, jj, 1)
+                    elif n - 2 >= n_groups - 4:
+                        if jj == 1:
+                            store(U, 0, 2)
                     elif whole and step == len(tiles) - 1:
                         store(tiles[0][0], 0, len(tiles))
                     elif not whole and jj == 1:

from contextlib import ExitStack

import concourse.mybir as mybir
from concourse.masks import make_identity

F32 = mybir.dt.float32
BF16 = mybir.dt.bfloat16
U32 = mybir.dt.uint32
U8 = mybir.dt.uint8
FP8X4 = mybir.dt.float8_e4m3fn_x4
ALU = mybir.AluOpType

P = 128
D = 512
H = D // 2
TOKENS = 8192
FLOPS = 2 * 2 * TOKENS * D * D

G_DT = F32

CHUNK_TILES = [2, 2, 4] + [8] * 7
GROUP_UNITS = [1, 1] + [2] * 14 + [1, 1]
BULK = 8
BULK_BUFS = 3
OUT_BUFS = 4
HEAD_LOADS = ["x0","wg","x1","y0","x2","wo","y1","x3","y2"]
TAIL_SPLIT = 2


def tile_multiscaleretention_pb_t_kernel(tc, x, y_norm, wg_w, wo_w, out):
    nc = tc.nc
    xf = x.flatten_outer_dims()
    yf = y_norm.flatten_outer_dims()
    of = out.flatten_outer_dims()

    chunk_start = []
    units = []
    t0 = 0
    for c, tiles in enumerate(CHUNK_TILES):
        chunk_start.append(t0)
        for j0 in range(0, tiles, 2):
            units.append((c, j0))
        t0 += P * tiles
    assert t0 == TOKENS
    last_unit_of_chunk = {}
    for U, (c, j0) in enumerate(units):
        last_unit_of_chunk[c] = U
    groups = []
    group_of = {}
    for size in GROUP_UNITS:
        first = sum(len(g) for g in groups)
        groups.append(list(range(first, first + size)))
        for U in groups[-1]:
            group_of[U] = (len(groups) - 1, U - first)
    assert sum(GROUP_UNITS) == len(units)
    n_groups = len(groups)

    def members(G):
        return groups[G] if 0 <= G < n_groups else []

    def dram_rows(flat, c):
        tiles = CHUNK_TILES[c]
        rows = flat[chunk_start[c] : chunk_start[c] + P * tiles, :]
        return rows.rearrange("(p j) d -> p j d", j=tiles)

    with ExitStack() as ctx:
        const = ctx.enter_context(tc.tile_pool(name="const", bufs=1))
        xin = ctx.enter_context(tc.tile_pool(name="xin", bufs=1))
        yin = ctx.enter_context(tc.tile_pool(name="yin", bufs=1))
        work = ctx.enter_context(tc.tile_pool(name="work", bufs=3))
        outp = ctx.enter_context(tc.tile_pool(name="outp", bufs=OUT_BUFS))
        psum = ctx.enter_context(tc.psum_pool(name="psum", bufs=2))
        ctx.enter_context(tc.manual_schedule())

        x_sb = {}
        y_sb = {}
        xt_ps = {}
        xg = {}
        xq = {}
        g_ps = {}
        h_sb = {}
        ht_ps = {}
        hg = {}
        hq = {}
        o_ps = {}
        o_sb = {}

        def load(pool, table, flat, c, letter):
            tiles = CHUNK_TILES[c]
            if tiles == BULK:
                t = pool.tile([P, tiles, D], BF16, name="%sb" % letter, tag="%sb" % letter, bufs=BULK_BUFS)
            else:
                t = pool.tile([P, tiles, D], BF16, name="%sh%d" % (letter, c), tag="%sh%d" % (letter, c), bufs=1)
            nc.sync.dma_start(out=t[:], in_=dram_rows(flat, c))
            table[c] = t

        def load_x(c):
            if c < len(CHUNK_TILES):
                load(xin, x_sb, xf, c, "x")

        def load_y(c):
            if c < len(CHUNK_TILES):
                load(yin, y_sb, yf, c, "y")

        def copy_on(engine, dst, src):
            if engine == "V":
                nc.vector.tensor_copy(out=dst, in_=src)
            else:
                nc.scalar.copy(out=dst, in_=src)

        def transpose_x(U):
            c, j0 = units[U]
            ps = psum.tile([P, 2, 2, P], F32, name="xt_ps", tag="bank", bufs=8)
            for jj in range(2):
                words = x_sb[c][:, j0 + jj, :].bitcast(F32)
                for u in range(2):
                    nc.tensor.transpose(ps[:, jj, u, :], words[:, u:H:2], ident[:])
            xt_ps[U] = ps
            if U == last_unit_of_chunk[c] and CHUNK_TILES[c] == BULK:
                load_x(c + BULK_BUFS)

        def ungroup(engine, ps, table, tag, U):
            G, k = group_of[U]
            if k == 0:
                table[G] = work.tile([P, len(groups[G]) * 8 * P], BF16, name=tag, tag=tag, bufs=3, align_bytes=64)
            copy_on(
                engine,
                table[G][:, k * 8 * P : (k + 1) * 8 * P].bitcast(F32).rearrange("p (j r u) -> p j r u", j=2, u=2),
                ps[:].rearrange("p j u r -> p j r u"),
            )

        def quantize(grouped, tag, G):
            width = len(groups[G]) * 2 * P
            codes = work.tile([P, width], U32, name=tag + "c", tag=tag + "c", bufs=3, align_bytes=64)
            scales = work.tile([P, width], U8, name=tag + "s", tag=tag + "s", bufs=3, align_bytes=64)
            nc.vector.quantize_mx(out=codes[:].bitcast(FP8X4), scales=scales[:], in_=grouped[:])
            return codes, scales

        def stage1(U, u):
            G, k = group_of[U]
            codes, scales = xq[G]
            g = psum.tile([P, 2, H], G_DT, name="g_ps", tag="bank", bufs=8)
            half = slice(u * H, (u + 1) * H)
            for jj in range(2):
                cols = slice((2 * k + jj) * P, (2 * k + jj + 1) * P)
                nc.tensor.matmul_mx(
                    out=g[:, jj, :],
                    lhsT=codes[:, cols].bitcast(FP8X4),
                    lhsT_scale=scales[:, cols],
                    rhs=wgc[:, half].bitcast(FP8X4),
                    rhs_scale=wgs[:, half],
                    start=True,
                    stop=True,
                )
            g_ps[(U, u)] = g

        def gate(U, u):
            c, j0 = units[U]
            if u == 0:
                h_sb[U] = work.tile([P, 2, D], BF16, name="h_sb", tag="h", bufs=5, align_bytes=64)
            y_pairs = (
                y_sb[c][:, j0 : j0 + 2, :]
                .rearrange("p j d -> p (j d)")
                .rearrange("p (m u e) -> p u m e", u=2, e=2)
            )
            nc.vector.scalar_tensor_tensor(
                out=h_sb[U][:, u, :].rearrange("p (m e) -> p m e", e=2),
                in0=g_ps[(U, u)][:].rearrange("p j d -> p (j d)").rearrange("p (m e) -> p m e", e=2),
                scalar=0.0,
                in1=y_pairs[:, u],
                op0=ALU.max,
                op1=ALU.mult,
            )
            if u == 1 and U == last_unit_of_chunk[c] and CHUNK_TILES[c] == BULK:
                load_y(c + BULK_BUFS)

        def transpose_h(U):
            ps = psum.tile([P, 2, 2, P], F32, name="ht_ps", tag="bank", bufs=8)
            for jj in range(2):
                for u in range(2):
                    words = h_sb[U][:, u, jj * H : (jj + 1) * H].bitcast(F32)
                    nc.tensor.transpose(ps[:, jj, u, :], words, ident[:])
            ht_ps[U] = ps

        def stage2(U, jj):
            G, k = group_of[U]
            codes, scales = hq[G]
            o = psum.tile([P, D], F32, name="o_ps", tag="bank", bufs=8)
            cols = slice((2 * k + jj) * P, (2 * k + jj + 1) * P)
            nc.tensor.matmul_mx(
                out=o[:],
                lhsT=codes[:, cols].bitcast(FP8X4),
                lhsT_scale=scales[:, cols],
                rhs=woc[:].bitcast(FP8X4),
                rhs_scale=wos[:],
                start=True,
                stop=True,
            )
            o_ps[(U, jj)] = o

        def copy_out(U, jj, engine):
            G, k = group_of[U]
            if k == 0 and jj == 0:
                o_sb[G] = outp.tile([P, 2 * len(groups[G]), D], F32, name="o_sb", tag="o_sb", bufs=OUT_BUFS)
            copy_on(engine, o_sb[G][:, 2 * k + jj, :], o_ps[(U, jj)][:])

        def store(U, jj, count):
            c, j0 = units[U]
            G, k = group_of[U]
            nc.sync.dma_start(
                out=dram_rows(of, c)[:, j0 + jj : j0 + jj + count, :],
                in_=o_sb[G][:, 2 * k + jj : 2 * k + jj + count, :],
            )

        wg_raw = const.tile([P, 4, D], BF16, name="wg_raw")
        wo_raw = const.tile([P, 4, D], BF16, name="wo_raw")
        for what in HEAD_LOADS:
            if what == "wg":
                nc.sync.dma_start(out=wg_raw[:], in_=wg_w.rearrange("(p j) c -> p j c", j=4))
            elif what == "wo":
                nc.sync.dma_start(out=wo_raw[:], in_=wo_w.rearrange("(p j) c -> p j c", j=4))
            elif what.startswith("x"):
                load_x(int(what[1:]))
            else:
                load_y(int(what[1:]))
        for c in range(CHUNK_TILES.index(BULK), CHUNK_TILES.index(BULK) + BULK_BUFS):
            if c not in x_sb:
                load_x(c)
            if c not in y_sb:
                load_y(c)

        ident = const.tile([P, P], F32, name="ident")
        make_identity(nc, ident[:])
        warm = const.tile([P, 2], F32, name="warm")
        nc.vector.memset(warm[:, 0:1], 0.0)
        nc.scalar.copy(out=warm[:, 1:2], in_=warm[:, 0:1])

        wg_grp = const.tile([P, 4 * D], BF16, name="wg_grp", align_bytes=64)
        wgc = const.tile([P, D], U32, name="wgc", align_bytes=64)
        wgs = const.tile([P, D], U8, name="wgs", align_bytes=64)
        wo_grp = const.tile([P, 4 * D], BF16, name="wo_grp", align_bytes=64)
        woc = const.tile([P, D], U32, name="woc", align_bytes=64)
        wos = const.tile([P, D], U8, name="wos", align_bytes=64)

        def group_wg(u, engine):
            copy_on(
                engine,
                wg_grp[:, u * 2 * D : (u + 1) * 2 * D].rearrange("p (q e j) -> p q e j", e=2, j=4),
                wg_raw[:].rearrange("p j (q u e) -> p u q e j", u=2, e=2)[:, u],
            )

        def quantize_wg(u):
            nc.vector.quantize_mx(
                out=wgc[:, u * H : (u + 1) * H].bitcast(FP8X4),
                scales=wgs[:, u * H : (u + 1) * H],
                in_=wg_grp[:, u * 2 * D : (u + 1) * 2 * D],
            )

        def group_wo(half, engine):
            copy_on(
                engine,
                wo_grp[:, half * 2 * D : (half + 1) * 2 * D].rearrange("p (n j) -> p n j", j=4),
                wo_raw[:, :, half * H : (half + 1) * H].rearrange("p j n -> p n j"),
            )

        for n in range(-1, n_groups + 2):
            if members(n):
                xq[n] = quantize(xg[n], "x", n)
            if n == 0:
                quantize_wg(0)
                quantize_wg(1)
            if n == 2:
                nc.vector.quantize_mx(out=woc[:].bitcast(FP8X4), scales=wos[:], in_=wo_grp[:])
            if members(n - 2):
                hq[n - 2] = quantize(hg[n - 2], "h", n - 2)
            nxt = members(n + 1)
            prv = members(n - 1)
            if nxt:
                transpose_x(nxt[0])
                ungroup("S", xt_ps[nxt[0]], xg, "xg", nxt[0])
            if n == -1:
                group_wg(0, "V")
                group_wg(1, "S")
            for U in prv:
                transpose_h(U)
                ungroup("V" if (U == prv[-1] and n > 3) else "S", ht_ps[U], hg, "hg", U)
            for U in nxt[1:]:
                transpose_x(U)
                ungroup("S", xt_ps[U], xg, "xg", U)
            if n == 1:
                group_wo(0, "S")
                group_wo(1, "V")
            banks = [(U, u) for U in members(n) for u in range(2)]
            tiles = [(U, jj) for U in members(n - 2) for jj in range(2)]
            drain = n - 2 >= n_groups - TAIL_SPLIT
            for step in range(max(len(banks), len(tiles))):
                if step < len(banks):
                    stage1(banks[step][0], banks[step][1])
                    gate(banks[step][0], banks[step][1])
                if step < len(tiles):
                    U, jj = tiles[step]
                    stage2(U, jj)
                    copy_out(U, jj, "V" if (drain and step % 2 == 1) else "S")
                    whole = units[tiles[0][0]][0] == units[tiles[-1][0]][0]
                    if n - 2 >= n_groups - 1:
                        store(U, jj, 1)
                    elif n - 2 >= n_groups - 4:
                        if jj == 1:
                            store(U, 0, 2)
                    elif whole and step == len(tiles) - 1:
                        store(tiles[0][0], 0, len(tiles))
                    elif not whole and jj == 1:
                        store(U, 0, 2)
